import numpy as np
import ml_dtypes


def mxq(x, axis, fmt="e4m3"):
    dtype, down = {"e4m3": (ml_dtypes.float8_e4m3fn, 7), "e5m2": (ml_dtypes.float8_e5m2, 14)}[fmt]
    v = np.moveaxis(np.asarray(x, np.float32).astype(ml_dtypes.bfloat16).astype(np.float64), axis, -1)
    blocks = v.reshape(v.shape[:-1] + (-1, 32))
    amax = np.abs(blocks).max(-1, keepdims=True)
    byte = np.maximum(np.where(amax > 0, np.frexp(amax)[1] - 1 + 127, 0) - down, 1)
    scale = np.exp2(byte - 127.0)
    codes = (blocks / scale).astype(np.float32).astype(dtype).astype(np.float64)
    return np.moveaxis((codes * scale).reshape(v.shape), -1, axis)


WIDE = False


def mx_kscale(k):
    if not WIDE:
        return np.ones(k)
    levels = np.array([10, -10, 5, -5, 0])
    a = np.random.permutation(np.resize(levels, k // 512 * 4)).reshape(k // 512, 4)
    idx = np.arange(k)
    return np.exp2(a[idx // 512, idx % 128 // 32])


BF16 = ml_dtypes.bfloat16


def bf(x):
    return np.asarray(x, np.float32).astype(BF16)


def f64(x):
    return np.asarray(x).astype(np.float64)


B, S, D, H = 1, 1024, 512, 512


def setup_inputs():
    s, t = mx_kscale(D), mx_kscale(H)
    return {"audio_feature": bf(np.random.standard_normal((B, S, D)) * s),
            "W_phi": bf(np.random.standard_normal((D, H)) / np.sqrt(D) / s[:, None] * t),
            "b_phi": bf(np.random.standard_normal(H) * 0.2 * t),
            "W_theta": bf(np.random.standard_normal((D, H)) / np.sqrt(D) / s[:, None] / t),
            "b_theta": bf(np.random.standard_normal(H) * 0.2 / t)}


def reference(audio_feature, W_phi, b_phi, W_theta, b_theta):
    xq = mxq(f64(audio_feature), 2, "e4m3")
    phi_a = (xq @ mxq(f64(W_phi), 0, "e4m3")) + f64(b_phi)
    theta_a = (xq @ mxq(f64(W_theta), 0, "e4m3")) + f64(b_theta)
    scores = (mxq(phi_a, 2, "e4m3") @ mxq(theta_a, 2, "e4m3").transpose(0, 2, 1)) / np.sqrt(D)
    scores = np.maximum(scores, 0.0)
    return (scores + scores.transpose(0, 2, 1)) * 0.5

@@ -1,0 +1,213 @@
+import math
+
+import concourse.mybir as mybir
+from concourse.masks import make_identity
+
+F32 = mybir.dt.float32
+BF16 = mybir.dt.bfloat16
+U32 = mybir.dt.uint32
+U8 = mybir.dt.uint8
+FP8X4 = mybir.dt.float8_e4m3fn_x4
+ACT = mybir.ActivationFunctionType
+ALU = mybir.AluOpType
+
+P = 128
+PACK = 4
+S = 1024
+D = 512
+H = 512
+BANK = 512
+HALVES = S // BANK
+TILES = BANK // P
+PAIR = 2 * P
+PAIRS = S // PAIR
+PHI = 0
+THETA = 1
+RESULT_SCALE = 0.5 / math.sqrt(D)
+
+FLOPS = 2 * (2 * S * D * H) + 2 * S * S * H
+
+
+def regroup(nc, grouped, planes):
+    nc.vector.tensor_copy(
+        out=grouped[:].rearrange("p (c i t) -> p c t i", i=4, t=PACK),
+        in_=planes[:].rearrange("p (t c i) -> p c t i", i=4, t=PACK),
+    )
+
+
+def tile_selfattention_pa_kernel(tc, audio_feature, W_phi, b_phi, W_theta, b_theta, out):
+    nc = tc.nc
+    x = audio_feature.flatten_outer_dims()
+    result = out.flatten_outer_dims()
+    weights = (W_phi, W_theta)
+    biases = (b_phi, b_theta)
+
+    with tc.tile_pool(name="keep", bufs=1) as keep, tc.psum_pool(name="psum", bufs=8) as psum:
+        identity = keep.tile([P, P], F32)
+        bias_rows = keep.tile([P, P], BF16)
+        bias_rows_f32 = keep.tile([P, P], F32)
+        bias_cols = keep.tile([P, 2 * PACK], F32)
+
+        x_raw = [keep.tile([P, 2 * D], BF16, name="x_raw%d" % g) for g in range(PAIRS)]
+        x_grouped = [
+            keep.tile([P, PAIR * PACK], BF16, name="x_grouped%d" % g, align_bytes=64) for g in range(PAIRS)
+        ]
+        x_codes = [keep.tile([P, BANK], U32, name="x_codes%d" % h, align_bytes=64) for h in range(HALVES)]
+        x_scales = [keep.tile([P, BANK], U8, name="x_scales%d" % h, align_bytes=64) for h in range(HALVES)]
+
+        w_raw = [keep.tile([P, PACK * H], BF16, name="w_raw%d" % o) for o in (PHI, THETA)]
+        w_grouped = [keep.tile([P, H * PACK], BF16, name="w_grouped%d" % o, align_bytes=64) for o in (PHI, THETA)]
+        w_codes = [keep.tile([P, H], U32, name="w_codes%d" % o, align_bytes=64) for o in (PHI, THETA)]
+        w_scales = [keep.tile([P, H], U8, name="w_scales%d" % o, align_bytes=64) for o in (PHI, THETA)]
+
+        proj_planes = [
+            [keep.tile([P, PACK * BANK], BF16, name="proj_planes%d_%d" % (o, h)) for h in range(HALVES)]
+            for o in (PHI, THETA)
+        ]
+        proj_grouped = [
+            [keep.tile([P, BANK * PACK], BF16, name="proj_grouped%d_%d" % (o, h), align_bytes=64) for h in range(HALVES)]
+            for o in (PHI, THETA)
+        ]
+        proj_codes = [
+            [keep.tile([P, BANK], U32, name="proj_codes%d_%d" % (o, h), align_bytes=64) for h in range(HALVES)]
+            for o in (PHI, THETA)
+        ]
+        proj_scales = [
+            [keep.tile([P, BANK], U8, name="proj_scales%d_%d" % (o, h), align_bytes=64) for h in range(HALVES)]
+            for o in (PHI, THETA)
+        ]
+
+        r_half = [
+            [keep.tile([P, BANK], F32, name="r_half%d_%d" % (i, h)) for h in range(HALVES)] for i in range(S // P)
+        ]
+        out_half = [
+            [keep.tile([P, BANK], F32, name="out_half%d_%d" % (i, h)) for h in range(HALVES)] for i in range(S // P)
+        ]
+
+        def load_x(g):
+            nc.sync.dma_start(
+                out=x_raw[g][:].rearrange("p (t d) -> p t d", t=2),
+                in_=x[g * PAIR : (g + 1) * PAIR, :].rearrange("(t p) d -> p t d", p=P),
+            )
+
+        def load_weight(o):
+            nc.sync.dma_start(
+                out=w_raw[o][:].rearrange("p (u e h) -> p u e h", u=2, e=2),
+                in_=weights[o].rearrange("(u q e) h -> q u e h", u=2, e=2),
+            )
+
+        def prepare_bias():
+            nc.vector.memset(bias_rows[:], 0.0)
+            for o in (PHI, THETA):
+                nc.scalar.dma_start(
+                    out=bias_rows[o * PACK : (o + 1) * PACK, :], in_=biases[o].rearrange("(j p) -> j p", p=P)
+                )
+            nc.vector.tensor_copy(out=bias_rows_f32[:], in_=bias_rows[:])
+            bank = psum.tile([P, BANK], F32, name="bank", tag="bank")
+            nc.tensor.transpose(bank[:, 0:P], bias_rows_f32[:], identity[:])
+            nc.vector.tensor_copy(out=bias_cols[:], in_=bank[:, 0 : 2 * PACK])
+
+        def quantise_weight(o):
+            regroup(nc, w_grouped[o], w_raw[o])
+            nc.vector.quantize_mx(out=w_codes[o][:].bitcast(FP8X4), scales=w_scales[o][:], in_=w_grouped[o][:])
+
+        def quantise_x(g):
+            words = x_raw[g][:].bitcast(F32)
+            bank = psum.tile([P, BANK], F32, name="bank", tag="bank")
+            for tu in range(2 * 2):
+                nc.tensor.transpose(bank[:, tu * P : (tu + 1) * P], words[:, tu * P : (tu + 1) * P], identity[:])
+            nc.scalar.copy(
+                out=x_grouped[g][:].bitcast(F32).rearrange("p (t s u) -> p t s u", t=2, u=2),
+                in_=bank[:].rearrange("p (t u s) -> p t s u", t=2, u=2),
+            )
+            half, cols = g // 2, slice((g % 2) * PAIR, (g % 2 + 1) * PAIR)
+            nc.vector.quantize_mx(
+                out=x_codes[half][:, cols].bitcast(FP8X4), scales=x_scales[half][:, cols], in_=x_grouped[g][:]
+            )
+
+        def project(o, half):
+            for j in range(PACK):
+                cols = slice(j * P, (j + 1) * P)
+                bank = psum.tile([P, BANK], F32, name="bank", tag="bank")
+                nc.tensor.matmul_mx(
+                    out=bank[:],
+                    lhsT=w_codes[o][:, cols].bitcast(FP8X4),
+                    lhsT_scale=w_scales[o][:, cols],
+                    rhs=x_codes[half][:].bitcast(FP8X4),
+                    rhs_scale=x_scales[half][:],
+                    start=True,
+                    stop=True,
+                )
+                nc.scalar.activation(
+                    out=proj_planes[o][half][:, j * BANK : (j + 1) * BANK],
+                    in_=bank[:],
+                    func=ACT.Identity,
+                    bias=bias_cols[:, o * PACK + j : o * PACK + j + 1],
+                    scale=1.0,
+                )
+            regroup(nc, proj_grouped[o][half], proj_planes[o][half])
+            nc.vector.quantize_mx(
+                out=proj_codes[o][half][:].bitcast(FP8X4),
+                scales=proj_scales[o][half][:],
+                in_=proj_grouped[o][half][:],
+            )
+
+        def scores(row_half, col_half):
+            for k in range(TILES):
+                cols = slice(k * P, (k + 1) * P)
+                bank = psum.tile([P, BANK], F32, name="bank", tag="bank")
+                nc.tensor.matmul_mx(
+                    out=bank[:],
+                    lhsT=proj_codes[PHI][row_half][:, cols].bitcast(FP8X4),
+                    lhsT_scale=proj_scales[PHI][row_half][:, cols],
+                    rhs=proj_codes[THETA][col_half][:].bitcast(FP8X4),
+                    rhs_scale=proj_scales[THETA][col_half][:],
+                    start=True,
+                    stop=True,
+                )
+                nc.scalar.activation(
+                    out=r_half[row_half * TILES + k][col_half][:], in_=bank[:], func=ACT.Relu, scale=RESULT_SCALE
+                )
+
+        def symmetrise(row_half, col_half):
+            for k in range(TILES):
+                i = row_half * TILES + k
+                bank = psum.tile([P, BANK], F32, name="bank", tag="bank")
+                for m in range(TILES):
+                    nc.tensor.transpose(
+                        bank[:, m * P : (m + 1) * P],
+                        r_half[col_half * TILES + m][row_half][:, k * P : (k + 1) * P],
+                        identity[:],
+                    )
+                nc.vector.tensor_tensor(out=out_half[i][col_half][:], in0=bank[:], in1=r_half[i][col_half][:], op=ALU.add)
+                nc.sync.dma_start(
+                    out=result[i * P : (i + 1) * P, col_half * BANK : (col_half + 1) * BANK], in_=out_half[i][col_half][:]
+                )
+
+        make_identity(nc, identity[:])
+        load_weight(PHI)
+        load_x(0)
+        load_x(1)
+        load_weight(THETA)
+        load_x(2)
+        load_x(3)
+        prepare_bias()
+
+        quantise_weight(PHI)
+        quantise_x(0)
+        quantise_x(1)
+        quantise_weight(THETA)
+        project(PHI, 0)
+        project(THETA, 0)
+        quantise_x(2)
+        quantise_x(3)
+        scores(0, 0)
+        project(PHI, 1)
+        project(THETA, 1)
+        symmetrise(0, 0)
+        scores(0, 1)
+        scores(1, 0)
+        scores(1, 1)
+        symmetrise(0, 1)
+        symmetrise(1, 0)
+        symmetrise(1, 1)

@@ -28,11 +28,22 @@ RESULT_SCALE = 0.5 / math.sqrt(D)
 FLOPS = 2 * (2 * S * D * H) + 2 * S * S * H
 
 
-def regroup(nc, grouped, planes):
-    nc.vector.tensor_copy(
-        out=grouped[:].rearrange("p (c i t) -> p c t i", i=4, t=PACK),
-        in_=planes[:].rearrange("p (t c i) -> p c t i", i=4, t=PACK),
-    )
+def regroup_and_quantise(nc, planes, grouped, codes, scales, pieces):
+    columns = codes.shape[1]
+    width = columns // pieces
+    source = planes[:].rearrange("p (t c i) -> p c t i", i=4, t=PACK)
+    target = grouped[:].rearrange("p (c i t) -> p c t i", i=4, t=PACK)
+    for piece in range(pieces + 1):
+        if piece < pieces:
+            runs = slice(piece * width // 4, (piece + 1) * width // 4)
+            nc.vector.tensor_copy(out=target[:, runs], in_=source[:, runs])
+        if piece > 0:
+            cols = slice((piece - 1) * width, piece * width)
+            nc.vector.quantize_mx(
+                out=codes[:, cols].bitcast(FP8X4),
+                scales=scales[:, cols],
+                in_=grouped[:, (piece - 1) * width * PACK : piece * width * PACK],
+            )
 
 
 def tile_selfattention_pa_kernel(tc, audio_feature, W_phi, b_phi, W_theta, b_theta, out):
@@ -96,22 +107,22 @@ def tile_selfattention_pa_kernel(tc, audio_feature, W_phi, b_phi, W_theta, b_the
                 in_=weights[o].rearrange("(u q e) h -> q u e h", u=2, e=2),
             )
 
-        def prepare_bias():
-            nc.vector.memset(bias_rows[:], 0.0)
+        def load_bias():
             for o in (PHI, THETA):
-                nc.scalar.dma_start(
+                nc.sync.dma_start(
                     out=bias_rows[o * PACK : (o + 1) * PACK, :], in_=biases[o].rearrange("(j p) -> j p", p=P)
                 )
+
+        def bias_to_columns():
             nc.vector.tensor_copy(out=bias_rows_f32[:], in_=bias_rows[:])
             bank = psum.tile([P, BANK], F32, name="bank", tag="bank")
             nc.tensor.transpose(bank[:, 0:P], bias_rows_f32[:], identity[:])
             nc.vector.tensor_copy(out=bias_cols[:], in_=bank[:, 0 : 2 * PACK])
 
         def quantise_weight(o):
-            regroup(nc, w_grouped[o], w_raw[o])
-            nc.vector.quantize_mx(out=w_codes[o][:].bitcast(FP8X4), scales=w_scales[o][:], in_=w_grouped[o][:])
+            regroup_and_quantise(nc, w_raw[o], w_grouped[o], w_codes[o], w_scales[o], pieces=H // P)
 
-        def quantise_x(g):
+        def transpose_x(g):
             words = x_raw[g][:].bitcast(F32)
             bank = psum.tile([P, BANK], F32, name="bank", tag="bank")
             for tu in range(2 * 2):
@@ -120,6 +131,8 @@ def tile_selfattention_pa_kernel(tc, audio_feature, W_phi, b_phi, W_theta, b_the
                 out=x_grouped[g][:].bitcast(F32).rearrange("p (t s u) -> p t s u", t=2, u=2),
                 in_=bank[:].rearrange("p (t u s) -> p t s u", t=2, u=2),
             )
+
+        def quantise_x(g):
             half, cols = g // 2, slice((g % 2) * PAIR, (g % 2 + 1) * PAIR)
             nc.vector.quantize_mx(
                 out=x_codes[half][:, cols].bitcast(FP8X4), scales=x_scales[half][:, cols], in_=x_grouped[g][:]
@@ -138,18 +151,16 @@ def tile_selfattention_pa_kernel(tc, audio_feature, W_phi, b_phi, W_theta, b_the
                     start=True,
                     stop=True,
                 )
-                nc.scalar.activation(
-                    out=proj_planes[o][half][:, j * BANK : (j + 1) * BANK],
-                    in_=bank[:],
-                    func=ACT.Identity,
-                    bias=bias_cols[:, o * PACK + j : o * PACK + j + 1],
-                    scale=1.0,
-                )
-            regroup(nc, proj_grouped[o][half], proj_planes[o][half])
-            nc.vector.quantize_mx(
-                out=proj_codes[o][half][:].bitcast(FP8X4),
-                scales=proj_scales[o][half][:],
-                in_=proj_grouped[o][half][:],
+                plane = proj_planes[o][half][:, j * BANK : (j + 1) * BANK]
+                bias = bias_cols[:, o * PACK + j : o * PACK + j + 1]
+                if o == THETA and j == PACK - 1:
+                    nc.vector.tensor_scalar(out=plane, in0=bank[:], scalar1=bias, scalar2=None, op0=ALU.add)
+                else:
+                    nc.scalar.activation(out=plane, in_=bank[:], func=ACT.Identity, bias=bias, scale=1.0)
+
+        def quantise_projection(o, half):
+            regroup_and_quantise(
+                nc, proj_planes[o][half], proj_grouped[o][half], proj_codes[o][half], proj_scales[o][half], pieces=2
             )
 
         def scores(row_half, col_half):
@@ -184,30 +195,43 @@ def tile_selfattention_pa_kernel(tc, audio_feature, W_phi, b_phi, W_theta, b_the
                     out=result[i * P : (i + 1) * P, col_half * BANK : (col_half + 1) * BANK], in_=out_half[i][col_half][:]
                 )
 
-        make_identity(nc, identity[:])
-        load_weight(PHI)
-        load_x(0)
-        load_x(1)
-        load_weight(THETA)
-        load_x(2)
-        load_x(3)
-        prepare_bias()
+        with tc.manual_schedule():
+            nc.vector.memset(bias_rows[:], 0.0)
+            make_identity(nc, identity[:])
+            load_x(0)
+            load_x(1)
+            load_bias()
+            load_weight(PHI)
+            load_x(2)
+            load_x(3)
+            load_weight(THETA)
 
-        quantise_weight(PHI)
-        quantise_x(0)
-        quantise_x(1)
-        quantise_weight(THETA)
-        project(PHI, 0)
-        project(THETA, 0)
-        quantise_x(2)
-        quantise_x(3)
-        scores(0, 0)
-        project(PHI, 1)
-        project(THETA, 1)
-        symmetrise(0, 0)
-        scores(0, 1)
-        scores(1, 0)
-        scores(1, 1)
-        symmetrise(0, 1)
-        symmetrise(1, 0)
-        symmetrise(1, 1)
+            transpose_x(0)
+            transpose_x(1)
+            bias_to_columns()
+            quantise_x(0)
+            quantise_x(1)
+            quantise_weight(PHI)
+            transpose_x(2)
+            transpose_x(3)
+            quantise_x(2)
+            quantise_x(3)
+
+            project(PHI, 0)
+            quantise_weight(THETA)
+            quantise_projection(PHI, 0)
+            project(THETA, 0)
+            project(PHI, 1)
+            quantise_projection(THETA, 0)
+            quantise_projection(PHI, 1)
+            project(THETA, 1)
+
+            scores(0, 0)
+            scores(1, 0)
+            quantise_projection(THETA, 1)
+            symmetrise(0, 0)
+            scores(0, 1)
+            symmetrise(0, 1)
+            scores(1, 1)
+            symmetrise(1, 0)
+            symmetrise(1, 1)

@@ -195,43 +195,42 @@ def tile_selfattention_pa_kernel(tc, audio_feature, W_phi, b_phi, W_theta, b_the
                     out=result[i * P : (i + 1) * P, col_half * BANK : (col_half + 1) * BANK], in_=out_half[i][col_half][:]
                 )
 
-        with tc.manual_schedule():
-            nc.vector.memset(bias_rows[:], 0.0)
-            make_identity(nc, identity[:])
-            load_x(0)
-            load_x(1)
-            load_bias()
-            load_weight(PHI)
-            load_x(2)
-            load_x(3)
-            load_weight(THETA)
+        nc.vector.memset(bias_rows[:], 0.0)
+        make_identity(nc, identity[:])
+        load_x(0)
+        load_x(1)
+        load_bias()
+        load_weight(PHI)
+        load_x(2)
+        load_x(3)
+        load_weight(THETA)
 
-            transpose_x(0)
-            transpose_x(1)
-            bias_to_columns()
-            quantise_x(0)
-            quantise_x(1)
-            quantise_weight(PHI)
-            transpose_x(2)
-            transpose_x(3)
-            quantise_x(2)
-            quantise_x(3)
+        transpose_x(0)
+        transpose_x(1)
+        bias_to_columns()
+        quantise_x(0)
+        quantise_x(1)
+        quantise_weight(PHI)
+        transpose_x(2)
+        transpose_x(3)
+        quantise_x(2)
+        quantise_x(3)
 
-            project(PHI, 0)
-            quantise_weight(THETA)
-            quantise_projection(PHI, 0)
-            project(THETA, 0)
-            project(PHI, 1)
-            quantise_projection(THETA, 0)
-            quantise_projection(PHI, 1)
-            project(THETA, 1)
+        project(PHI, 0)
+        quantise_weight(THETA)
+        quantise_projection(PHI, 0)
+        project(THETA, 0)
+        project(PHI, 1)
+        quantise_projection(THETA, 0)
+        quantise_projection(PHI, 1)
+        project(THETA, 1)
 
-            scores(0, 0)
-            scores(1, 0)
-            quantise_projection(THETA, 1)
-            symmetrise(0, 0)
-            scores(0, 1)
-            symmetrise(0, 1)
-            scores(1, 1)
-            symmetrise(1, 0)
-            symmetrise(1, 1)
+        scores(0, 0)
+        scores(1, 0)
+        quantise_projection(THETA, 1)
+        symmetrise(0, 0)
+        scores(0, 1)
+        symmetrise(0, 1)
+        scores(1, 1)
+        symmetrise(1, 0)
+        symmetrise(1, 1)

import math

import concourse.mybir as mybir
from concourse.masks import make_identity

F32 = mybir.dt.float32
BF16 = mybir.dt.bfloat16
U32 = mybir.dt.uint32
U8 = mybir.dt.uint8
FP8X4 = mybir.dt.float8_e4m3fn_x4
ACT = mybir.ActivationFunctionType
ALU = mybir.AluOpType

P = 128
PACK = 4
S = 1024
D = 512
H = 512
BANK = 512
HALVES = S // BANK
TILES = BANK // P
PAIR = 2 * P
PAIRS = S // PAIR
PHI = 0
THETA = 1
RESULT_SCALE = 0.5 / math.sqrt(D)

FLOPS = 2 * (2 * S * D * H) + 2 * S * S * H


def regroup_and_quantise(nc, planes, grouped, codes, scales, pieces):
    columns = codes.shape[1]
    width = columns // pieces
    source = planes[:].rearrange("p (t c i) -> p c t i", i=4, t=PACK)
    target = grouped[:].rearrange("p (c i t) -> p c t i", i=4, t=PACK)
    for piece in range(pieces + 1):
        if piece < pieces:
            runs = slice(piece * width // 4, (piece + 1) * width // 4)
            nc.vector.tensor_copy(out=target[:, runs], in_=source[:, runs])
        if piece > 0:
            cols = slice((piece - 1) * width, piece * width)
            nc.vector.quantize_mx(
                out=codes[:, cols].bitcast(FP8X4),
                scales=scales[:, cols],
                in_=grouped[:, (piece - 1) * width * PACK : piece * width * PACK],
            )


def tile_selfattention_pa_kernel(tc, audio_feature, W_phi, b_phi, W_theta, b_theta, out):
    nc = tc.nc
    x = audio_feature.flatten_outer_dims()
    result = out.flatten_outer_dims()
    weights = (W_phi, W_theta)
    biases = (b_phi, b_theta)

    with tc.tile_pool(name="keep", bufs=1) as keep, tc.psum_pool(name="psum", bufs=8) as psum:
        identity = keep.tile([P, P], F32)
        bias_rows = keep.tile([P, P], BF16)
        bias_rows_f32 = keep.tile([P, P], F32)
        bias_cols = keep.tile([P, 2 * PACK], F32)

        x_raw = [keep.tile([P, 2 * D], BF16, name="x_raw%d" % g) for g in range(PAIRS)]
        x_grouped = [
            keep.tile([P, PAIR * PACK], BF16, name="x_grouped%d" % g, align_bytes=64) for g in range(PAIRS)
        ]
        x_codes = [keep.tile([P, BANK], U32, name="x_codes%d" % h, align_bytes=64) for h in range(HALVES)]
        x_scales = [keep.tile([P, BANK], U8, name="x_scales%d" % h, align_bytes=64) for h in range(HALVES)]

        w_raw = [keep.tile([P, PACK * H], BF16, name="w_raw%d" % o) for o in (PHI, THETA)]
        w_grouped = [keep.tile([P, H * PACK], BF16, name="w_grouped%d" % o, align_bytes=64) for o in (PHI, THETA)]
        w_codes = [keep.tile([P, H], U32, name="w_codes%d" % o, align_bytes=64) for o in (PHI, THETA)]
        w_scales = [keep.tile([P, H], U8, name="w_scales%d" % o, align_bytes=64) for o in (PHI, THETA)]

        proj_planes = [
            [keep.tile([P, PACK * BANK], BF16, name="proj_planes%d_%d" % (o, h)) for h in range(HALVES)]
            for o in (PHI, THETA)
        ]
        proj_grouped = [
            [keep.tile([P, BANK * PACK], BF16, name="proj_grouped%d_%d" % (o, h), align_bytes=64) for h in range(HALVES)]
            for o in (PHI, THETA)
        ]
        proj_codes = [
            [keep.tile([P, BANK], U32, name="proj_codes%d_%d" % (o, h), align_bytes=64) for h in range(HALVES)]
            for o in (PHI, THETA)
        ]
        proj_scales = [
            [keep.tile([P, BANK], U8, name="proj_scales%d_%d" % (o, h), align_bytes=64) for h in range(HALVES)]
            for o in (PHI, THETA)
        ]

        r_half = [
            [keep.tile([P, BANK], F32, name="r_half%d_%d" % (i, h)) for h in range(HALVES)] for i in range(S // P)
        ]
        out_half = [
            [keep.tile([P, BANK], F32, name="out_half%d_%d" % (i, h)) for h in range(HALVES)] for i in range(S // P)
        ]

        def load_x(g):
            nc.sync.dma_start(
                out=x_raw[g][:].rearrange("p (t d) -> p t d", t=2),
                in_=x[g * PAIR : (g + 1) * PAIR, :].rearrange("(t p) d -> p t d", p=P),
            )

        def load_weight(o):
            nc.sync.dma_start(
                out=w_raw[o][:].rearrange("p (u e h) -> p u e h", u=2, e=2),
                in_=weights[o].rearrange("(u q e) h -> q u e h", u=2, e=2),
            )

        def load_bias():
            for o in (PHI, THETA):
                nc.sync.dma_start(
                    out=bias_rows[o * PACK : (o + 1) * PACK, :], in_=biases[o].rearrange("(j p) -> j p", p=P)
                )

        def bias_to_columns():
            nc.vector.tensor_copy(out=bias_rows_f32[:], in_=bias_rows[:])
            bank = psum.tile([P, BANK], F32, name="bank", tag="bank")
            nc.tensor.transpose(bank[:, 0:P], bias_rows_f32[:], identity[:])
            nc.vector.tensor_copy(out=bias_cols[:], in_=bank[:, 0 : 2 * PACK])

        def quantise_weight(o):
            regroup_and_quantise(nc, w_raw[o], w_grouped[o], w_codes[o], w_scales[o], pieces=H // P)

        def transpose_x(g):
            words = x_raw[g][:].bitcast(F32)
            bank = psum.tile([P, BANK], F32, name="bank", tag="bank")
            for tu in range(2 * 2):
                nc.tensor.transpose(bank[:, tu * P : (tu + 1) * P], words[:, tu * P : (tu + 1) * P], identity[:])
            nc.scalar.copy(
                out=x_grouped[g][:].bitcast(F32).rearrange("p (t s u) -> p t s u", t=2, u=2),
                in_=bank[:].rearrange("p (t u s) -> p t s u", t=2, u=2),
            )

        def quantise_x(g):
            half, cols = g // 2, slice((g % 2) * PAIR, (g % 2 + 1) * PAIR)
            nc.vector.quantize_mx(
                out=x_codes[half][:, cols].bitcast(FP8X4), scales=x_scales[half][:, cols], in_=x_grouped[g][:]
            )

        def project(o, half):
            for j in range(PACK):
                cols = slice(j * P, (j + 1) * P)
                bank = psum.tile([P, BANK], F32, name="bank", tag="bank")
                nc.tensor.matmul_mx(
                    out=bank[:],
                    lhsT=w_codes[o][:, cols].bitcast(FP8X4),
                    lhsT_scale=w_scales[o][:, cols],
                    rhs=x_codes[half][:].bitcast(FP8X4),
                    rhs_scale=x_scales[half][:],
                    start=True,
                    stop=True,
                )
                plane = proj_planes[o][half][:, j * BANK : (j + 1) * BANK]
                bias = bias_cols[:, o * PACK + j : o * PACK + j + 1]
                if o == THETA and j == PACK - 1:
                    nc.vector.tensor_scalar(out=plane, in0=bank[:], scalar1=bias, scalar2=None, op0=ALU.add)
                else:
                    nc.scalar.activation(out=plane, in_=bank[:], func=ACT.Identity, bias=bias, scale=1.0)

        def quantise_projection(o, half):
            regroup_and_quantise(
                nc, proj_planes[o][half], proj_grouped[o][half], proj_codes[o][half], proj_scales[o][half], pieces=2
            )

        def scores(row_half, col_half):
            for k in range(TILES):
                cols = slice(k * P, (k + 1) * P)
                bank = psum.tile([P, BANK], F32, name="bank", tag="bank")
                nc.tensor.matmul_mx(
                    out=bank[:],
                    lhsT=proj_codes[PHI][row_half][:, cols].bitcast(FP8X4),
                    lhsT_scale=proj_scales[PHI][row_half][:, cols],
                    rhs=proj_codes[THETA][col_half][:].bitcast(FP8X4),
                    rhs_scale=proj_scales[THETA][col_half][:],
                    start=True,
                    stop=True,
                )
                nc.scalar.activation(
                    out=r_half[row_half * TILES + k][col_half][:], in_=bank[:], func=ACT.Relu, scale=RESULT_SCALE
                )

        def symmetrise(row_half, col_half):
            for k in range(TILES):
                i = row_half * TILES + k
                bank = psum.tile([P, BANK], F32, name="bank", tag="bank")
                for m in range(TILES):
                    nc.tensor.transpose(
                        bank[:, m * P : (m + 1) * P],
                        r_half[col_half * TILES + m][row_half][:, k * P : (k + 1) * P],
                        identity[:],
                    )
                nc.vector.tensor_tensor(out=out_half[i][col_half][:], in0=bank[:], in1=r_half[i][col_half][:], op=ALU.add)
                nc.sync.dma_start(
                    out=result[i * P : (i + 1) * P, col_half * BANK : (col_half + 1) * BANK], in_=out_half[i][col_half][:]
                )

        nc.vector.memset(bias_rows[:], 0.0)
        make_identity(nc, identity[:])
        load_x(0)
        load_x(1)
        load_bias()
        load_weight(PHI)
        load_x(2)
        load_x(3)
        load_weight(THETA)

        transpose_x(0)
        transpose_x(1)
        bias_to_columns()
        quantise_x(0)
        quantise_x(1)
        quantise_weight(PHI)
        transpose_x(2)
        transpose_x(3)
        quantise_x(2)
        quantise_x(3)

        project(PHI, 0)
        quantise_weight(THETA)
        quantise_projection(PHI, 0)
        project(THETA, 0)
        project(PHI, 1)
        quantise_projection(THETA, 0)
        quantise_projection(PHI, 1)
        project(THETA, 1)

        scores(0, 0)
        scores(1, 0)
        quantise_projection(THETA, 1)
        symmetrise(0, 0)
        scores(0, 1)
        symmetrise(0, 1)
        scores(1, 1)
        symmetrise(1, 0)
        symmetrise(1, 1)
